import numpy as np
import ml_dtypes


def mxq(x, axis, fmt="e4m3"):
    dtype, down = {"e4m3": (ml_dtypes.float8_e4m3fn, 7), "e5m2": (ml_dtypes.float8_e5m2, 14)}[fmt]
    v = np.moveaxis(np.asarray(x, np.float32).astype(ml_dtypes.bfloat16).astype(np.float64), axis, -1)
    blocks = v.reshape(v.shape[:-1] + (-1, 32))
    amax = np.abs(blocks).max(-1, keepdims=True)
    byte = np.maximum(np.where(amax > 0, np.frexp(amax)[1] - 1 + 127, 0) - down, 1)
    scale = np.exp2(byte - 127.0)
    codes = (blocks / scale).astype(np.float32).astype(dtype).astype(np.float64)
    return np.moveaxis((codes * scale).reshape(v.shape), -1, axis)


WIDE = False


def mx_kscale(k):
    if not WIDE:
        return np.ones(k)
    levels = np.array([10, -10, 5, -5, 0])
    a = np.random.permutation(np.resize(levels, k // 512 * 4)).reshape(k // 512, 4)
    idx = np.arange(k)
    return np.exp2(a[idx // 512, idx % 128 // 32])


BF16 = ml_dtypes.bfloat16


def bf(x):
    return np.asarray(x, np.float32).astype(BF16)


def f64(x):
    return np.asarray(x).astype(np.float64)


E2M1 = np.array([0.0, 0.5, 1.0, 1.5, 2.0, 3.0, 4.0, 6.0, -0.0, -0.5, -1.0, -1.5, -2.0, -3.0, -4.0, -6.0])


def pack_weight(w, fmt):
    k, n = w.shape
    w = f64(bf(w)).reshape(k // 32, 32, n)
    amax = np.abs(w).max(1)
    if fmt == "e4m3":
        byte = np.frexp(amax)[1] - 1 + 127 - 7
    else:
        mant, ex = np.frexp(amax / 6.0)
        byte = np.where(mant > 0.5, ex, ex - 1) + 127
    byte = np.clip(np.where(amax > 0, byte, 1), 1, 254)
    scaled = (w * np.exp2(127.0 - byte)[:, None, :]).reshape(k, n).astype(np.float32)
    by_word = np.ascontiguousarray(scaled.reshape(k // 512, 128, 4, n).transpose(0, 1, 3, 2))
    if fmt == "e4m3":
        words = by_word.astype(ml_dtypes.float8_e4m3fn).view(np.uint8)
    else:
        c = by_word.astype(ml_dtypes.float4_e2m1fn).view(np.uint8) & 0xF
        words = c[..., 0::2] | (c[..., 1::2] << 4)
    return np.ascontiguousarray(words), np.ascontiguousarray(byte.astype(np.uint8).reshape(k // 512, 16, n))


def unpack_weight(words, scales, fmt):
    g, p, n, _ = words.shape
    if fmt == "e4m3":
        vals = np.ascontiguousarray(words).view(ml_dtypes.float8_e4m3fn).astype(np.float64)
    else:
        nib = np.empty((g, p, n, 4), np.uint8)
        nib[..., 0::2] = words & 0xF
        nib[..., 1::2] = words >> 4
        vals = E2M1[nib]
    vals = vals * np.repeat(np.exp2(scales.astype(np.float64) - 127.0), 8, axis=1)[..., None]
    return vals.transpose(0, 1, 3, 2).reshape(g * 512, n)


B, S, D, H, QL, KL, ND, VD, RD = 4, 256, 2048, 16, 512, 512, 128, 128, 128
QH = ND + RD
BASE = 10000.0


def rope(v):
    d = v.shape[-1]
    inv_freq = BASE ** (-np.arange(0, d, 2) / d)
    ang = np.arange(v.shape[1])[:, None] * inv_freq[None, :]
    cos = np.cos(ang)[None, :, None, :]
    sin = np.sin(ang)[None, :, None, :]
    v1 = v[..., 0::2]
    v2 = v[..., 1::2]
    o1 = v1 * cos - v2 * sin
    o2 = v1 * sin + v2 * cos
    return np.stack([o1, o2], axis=-1).reshape(v.shape)


def setup_inputs():
    s, t = mx_kscale(D), mx_kscale(QL)
    x = bf(np.random.standard_normal((B, S, D)) * s)
    Wqa_words, Wqa_scales = pack_weight(np.random.standard_normal((D, QL)) / np.sqrt(D) / s[:, None] * t, "e4m3")
    Wqb_words, Wqb_scales = pack_weight(np.random.standard_normal((QL, H * QH)) / np.sqrt(QL) / t[:, None], "e4m3")
    return {"x": x,
            "Wqa_words": Wqa_words, "Wqa_scales": Wqa_scales,
            "Wqb_words": Wqb_words, "Wqb_scales": Wqb_scales}


def reference(x, Wqa_words, Wqa_scales, Wqb_words, Wqb_scales):
    cq = mxq(f64(x), 2, "e4m3") @ unpack_weight(Wqa_words, Wqa_scales, "e4m3")
    q = (mxq(cq, 2, "e4m3") @ unpack_weight(Wqb_words, Wqb_scales, "e4m3")).reshape(B, S, H, QH)
    q_nope, q_pe = q[..., :ND], q[..., ND:]
    return np.concatenate([q_nope, rope(q_pe)], axis=-1)

@@ -1,0 +1,269 @@
+import math
+from contextlib import ExitStack
+
+import concourse.mybir as mybir
+from concourse.masks import make_identity
+
+F32 = mybir.dt.float32
+BF16 = mybir.dt.bfloat16
+I32 = mybir.dt.int32
+U32 = mybir.dt.uint32
+U8 = mybir.dt.uint8
+FP8X4 = mybir.dt.float8_e4m3fn_x4
+ALU = mybir.AluOpType
+ACT = mybir.ActivationFunctionType
+
+P = 128
+PACK = 4
+K_PASS = P * PACK
+
+TOKENS, D, QL = 1024, 2048, 512
+HEADS, ND, RD = 16, 128, 128
+QH = ND + RD
+SEQ = 256
+BASE = 10000.0
+
+TOKEN_TILES = TOKENS // P
+PASSES_A = D // K_PASS
+GROUP_HEADS = 4
+HEAD_GROUPS = HEADS // GROUP_HEADS
+GROUP_COLS = GROUP_HEADS * QH
+PAIRS = RD // 2
+LOOKAHEAD = 2
+
+TWO_PI = 2.0 * math.pi
+ROUND_MAGIC = 1.5 * 2.0**23
+
+FLOPS = 2 * TOKENS * D * QL + 2 * TOKENS * QL * HEADS * QH
+
+
+def build_rope_table(nc, pool, table):
+    position_int = pool.tile([P, 2], I32)
+    nc.gpsimd.iota(position_int[:], pattern=[[P, 2]], base=0, channel_multiplier=1)
+    position = pool.tile([P, 2], F32)
+    nc.vector.tensor_copy(out=position[:], in_=position_int[:])
+
+    freq = pool.tile([P, PAIRS], F32)
+    nc.vector.memset(freq[:], 1.0)
+    step = 1
+    while step < PAIRS:
+        bit_set = freq[:].rearrange("p (a two c) -> p a two c", two=2, c=step)[:, :, 1, :]
+        nc.vector.tensor_scalar_mul(out=bit_set, in0=bit_set, scalar1=BASE ** (-2.0 * step / RD))
+        step *= 2
+
+    turns = pool.tile([P, 2, PAIRS], F32)
+    for half in range(2):
+        nc.vector.tensor_scalar(
+            out=turns[:, half, :],
+            in0=freq[:],
+            scalar1=position[:, half : half + 1],
+            scalar2=1.0 / TWO_PI,
+            op0=ALU.mult,
+            op1=ALU.mult,
+        )
+
+    shifted = pool.tile([P, 2, 2, PAIRS, 2], F32)
+    nc.vector.tensor_copy(out=shifted[:, :, 0, :, 0], in_=turns[:])
+    nc.vector.tensor_scalar_add(out=shifted[:, :, 0, :, 1], in0=turns[:], scalar1=-0.25)
+    nc.vector.tensor_scalar_add(out=shifted[:, :, 1, :, 0], in0=turns[:], scalar1=0.25)
+    nc.vector.tensor_copy(out=shifted[:, :, 1, :, 1], in_=turns[:])
+    shifted_flat = shifted[:].rearrange("p a b j e -> p (a b j e)")
+
+    width = 2 * 2 * PAIRS * 2
+    whole = pool.tile([P, width], F32)
+    nc.vector.tensor_scalar(
+        out=whole[:], in0=shifted_flat, scalar1=ROUND_MAGIC, scalar2=ROUND_MAGIC, op0=ALU.add, op1=ALU.subtract
+    )
+    part = pool.tile([P, width], F32)
+    nc.vector.tensor_tensor(out=part[:], in0=shifted_flat, in1=whole[:], op=ALU.subtract)
+    minus_abs = pool.tile([P, width], F32)
+    nc.vector.scalar_tensor_tensor(
+        out=minus_abs[:], in0=part[:], scalar=-1.0, in1=part[:], op0=ALU.mult, op1=ALU.min
+    )
+    quarter_less = pool.tile([P, width], F32)
+    nc.vector.tensor_scalar_add(out=quarter_less[:], in0=minus_abs[:], scalar1=0.25)
+    nc.scalar.activation(
+        out=table[:].rearrange("p a b j e -> p (a b j e)"), in_=quarter_less[:], func=ACT.Sin, scale=TWO_PI
+    )
+
+
+def tile_multilatentattention_pa_kernel(tc, x, Wqa_words, Wqa_scales, Wqb_words, Wqb_scales, out):
+    nc = tc.nc
+    x_rows = x.rearrange("b s d -> (b s) d")
+    out_rows = out.rearrange("b s h f -> (b s) (h f)")
+
+    with ExitStack() as ctx:
+        consts = ctx.enter_context(tc.tile_pool(name="consts", bufs=1))
+        grouped_pool = ctx.enter_context(tc.tile_pool(name="grouped", bufs=2))
+        codes_pool = ctx.enter_context(tc.tile_pool(name="codes", bufs=LOOKAHEAD + 1))
+        rotate_pool = ctx.enter_context(tc.tile_pool(name="rotate", bufs=3))
+        stage_pool = ctx.enter_context(tc.tile_pool(name="stage", bufs=6))
+        psum_x = ctx.enter_context(tc.psum_pool(name="psum_x", bufs=2))
+        psum_cq = ctx.enter_context(tc.psum_pool(name="psum_cq", bufs=1))
+        psum_nope = ctx.enter_context(tc.psum_pool(name="psum_nope", bufs=2))
+        psum_rope = ctx.enter_context(tc.psum_pool(name="psum_rope", bufs=3))
+
+        wqa_planes = consts.tile([P, QL], U8, align_bytes=64)
+        wqb_planes = consts.tile([P, GROUP_COLS], U8, align_bytes=64)
+        nc.vector.memset(wqa_planes[:].bitcast(I32), 0)
+        nc.vector.memset(wqb_planes[:].bitcast(I32), 0)
+        wqa_words = consts.tile([P, PASSES_A, QL], U32, align_bytes=64)
+        wqb_words = consts.tile([P, HEADS * QH], U32, align_bytes=64)
+        x_sb = []
+        for i in range(TOKEN_TILES):
+            x_tile = consts.tile([P, D], BF16, name="x_sb%d" % i)
+            x_sb.append(x_tile)
+
+        def load_x(i):
+            nc.sync.dma_start(out=x_sb[i][:], in_=x_rows[i * P : (i + 1) * P, :])
+
+        def load_wqb(hg):
+            cols = slice(hg * GROUP_COLS, (hg + 1) * GROUP_COLS)
+            nc.sync.dma_start(
+                out=wqb_words[:, cols].bitcast(I32),
+                in_=Wqb_words[0].rearrange("p n t -> p (n t)").bitcast(I32)[:, cols],
+            )
+
+        load_x(0)
+        for quadrant in range(4):
+            rows = slice(4 * quadrant, 4 * quadrant + 4)
+            live = slice(32 * quadrant, 32 * quadrant + 16)
+            nc.sync.dma_start(out=wqa_planes[live, :].bitcast(I32), in_=Wqa_scales[:, rows, :].bitcast(I32))
+        for quadrant in range(4):
+            rows = slice(4 * quadrant, 4 * quadrant + 4)
+            live = slice(32 * quadrant, 32 * quadrant + 16)
+            nc.sync.dma_start(
+                out=wqb_planes[live, :].bitcast(I32),
+                in_=Wqb_scales[0, rows, :].rearrange("r (c n) -> c r n", c=HEAD_GROUPS).bitcast(I32),
+            )
+        nc.sync.dma_start(
+            out=wqa_words[:].bitcast(I32), in_=Wqa_words.rearrange("g p n t -> p g (n t)").bitcast(I32)
+        )
+        load_x(1)
+        load_wqb(0)
+        load_x(2)
+        for hg in range(1, HEAD_GROUPS):
+            load_wqb(hg)
+        for i in range(3, TOKEN_TILES):
+            load_x(i)
+
+        ident_f32 = consts.tile([P, P], F32)
+        make_identity(nc, ident_f32[:])
+        ident_bf16 = consts.tile([P, P], BF16)
+        make_identity(nc, ident_bf16[:])
+        table = consts.tile([P, 2, 2, PAIRS, 2], F32)
+        build_rope_table(nc, consts, table)
+
+        def front(i):
+            x_words = x_sb[i][:].bitcast(F32)
+            x_grouped = grouped_pool.tile([P, PASSES_A, P, PACK], BF16, align_bytes=64)
+            x_grouped_words = (
+                x_grouped[:]
+                .rearrange("p g r t -> p (g r t)")
+                .bitcast(F32)
+                .rearrange("p (g r u) -> p g r u", g=PASSES_A, u=2)
+            )
+            for first in range(0, PASSES_A, 2):
+                xt = psum_x.tile([P, 2, 2, P], F32)
+                for gg in range(2):
+                    start_word = (first + gg) * (K_PASS // 2)
+                    for u in range(2):
+                        nc.tensor.transpose(
+                            xt[:, gg, u, :],
+                            x_words[:, start_word + u : start_word + K_PASS // 2 : 2],
+                            ident_f32[:],
+                        )
+                nc.scalar.copy(
+                    out=x_grouped_words[:, first : first + 2, :, :], in_=xt[:].rearrange("p g u r -> p g r u")
+                )
+            x_codes = codes_pool.tile([P, PASSES_A * P], U32, align_bytes=64)
+            x_scales = codes_pool.tile([P, PASSES_A * P], U8, align_bytes=64)
+            nc.vector.quantize_mx(
+                out=x_codes[:].bitcast(FP8X4),
+                scales=x_scales[:],
+                in_=x_grouped[:].rearrange("p g r t -> p (g r t)"),
+            )
+
+            cq_ps = psum_cq.tile([P, QL], F32, tag="cq")
+            for g in range(PASSES_A):
+                tokens = slice(g * P, (g + 1) * P)
+                nc.tensor.matmul_mx(
+                    out=cq_ps[:],
+                    lhsT=x_codes[:, tokens].bitcast(FP8X4),
+                    lhsT_scale=x_scales[:, tokens],
+                    rhs=wqa_words[:, g, :].bitcast(FP8X4),
+                    rhs_scale=wqa_planes[4 * g : P, :],
+                    start=(g == 0),
+                    stop=(g == PASSES_A - 1),
+                )
+            cq_bf16 = grouped_pool.tile([P, PACK, P], BF16)
+            nc.scalar.copy(out=cq_bf16[:], in_=cq_ps[:].rearrange("p (c t) -> p t c", t=PACK))
+            cqT_ps = psum_cq.tile([P, PACK, P], BF16, tag="cq")
+            for t in range(PACK):
+                nc.tensor.transpose(cqT_ps[:, t, :], cq_bf16[:, t, :], ident_bf16[:])
+            cq_grouped = grouped_pool.tile([P, P, PACK], BF16, align_bytes=64)
+            nc.scalar.copy(out=cq_grouped[:], in_=cqT_ps[:].rearrange("p t r -> p r t"))
+            cq_codes = codes_pool.tile([P, P], U32, align_bytes=64)
+            cq_scales = codes_pool.tile([P, P], U8, align_bytes=64)
+            nc.vector.quantize_mx(
+                out=cq_codes[:].bitcast(FP8X4),
+                scales=cq_scales[:],
+                in_=cq_grouped[:].rearrange("p r t -> p (r t)"),
+            )
+            return cq_codes, cq_scales
+
+        def back(i, hg, cq_codes, cq_scales):
+            half = i % (SEQ // P)
+            rope_ps = psum_rope.tile([P, GROUP_HEADS, RD], F32)
+            nope_ps = psum_nope.tile([P, GROUP_HEADS, ND], F32)
+            for bank, offset in ((rope_ps, ND), (nope_ps, 0)):
+                for hh in range(GROUP_HEADS):
+                    first = hh * QH + offset
+                    nc.tensor.matmul_mx(
+                        out=bank[:, hh, :],
+                        lhsT=cq_codes[:].bitcast(FP8X4),
+                        lhsT_scale=cq_scales[:],
+                        rhs=wqb_words[:, hg * GROUP_COLS + first : hg * GROUP_COLS + first + P].bitcast(FP8X4),
+                        rhs_scale=wqb_planes[4 * hg : P, first : first + P],
+                        start=True,
+                        stop=True,
+                    )
+            stage = stage_pool.tile([P, GROUP_HEADS, QH], F32)
+            nc.scalar.copy(out=stage[:, :, 0:ND], in_=nope_ps[:])
+
+            shape = [P, GROUP_HEADS, PAIRS, 2]
+            pairs = rope_ps[:].rearrange("p h (j e) -> p h j e", e=2)
+            from_u = rotate_pool.tile(shape, F32)
+            from_w = rotate_pool.tile(shape, F32)
+            nc.vector.tensor_tensor(
+                out=from_u[:],
+                in0=pairs[:, :, :, 0:1].to_broadcast(shape),
+                in1=table[:, half, 0, :, :].unsqueeze(1).to_broadcast(shape),
+                op=ALU.mult,
+            )
+            nc.vector.tensor_tensor(
+                out=from_w[:],
+                in0=pairs[:, :, :, 1:2].to_broadcast(shape),
+                in1=table[:, half, 1, :, :].unsqueeze(1).to_broadcast(shape),
+                op=ALU.mult,
+            )
+            nc.gpsimd.tensor_tensor(
+                out=stage[:, :, ND:QH].rearrange("p h (j e) -> p h j e", e=2),
+                in0=from_u[:],
+                in1=from_w[:],
+                op=ALU.add,
+            )
+            nc.sync.dma_start(
+                out=out_rows[i * P : (i + 1) * P, hg * GROUP_COLS : (hg + 1) * GROUP_COLS],
+                in_=stage[:].rearrange("p h f -> p (h f)"),
+            )
+
+        ready = []
+        for i in range(LOOKAHEAD):
+            ready.append(front(i))
+        for i in range(TOKEN_TILES):
+            if i + LOOKAHEAD < TOKEN_TILES:
+                ready.append(front(i + LOOKAHEAD))
+            cq_codes, cq_scales = ready[i]
+            for hg in range(HEAD_GROUPS):
+                back(i, hg, cq_codes, cq_scales)

@@ -29,7 +29,7 @@ GROUP_HEADS = 4
 HEAD_GROUPS = HEADS // GROUP_HEADS
 GROUP_COLS = GROUP_HEADS * QH
 PAIRS = RD // 2
-LOOKAHEAD = 2
+LEAD = 3
 
 TWO_PI = 2.0 * math.pi
 ROUND_MAGIC = 1.5 * 2.0**23
@@ -37,7 +37,7 @@ ROUND_MAGIC = 1.5 * 2.0**23
 FLOPS = 2 * TOKENS * D * QL + 2 * TOKENS * QL * HEADS * QH
 
 
-def build_rope_table(nc, pool, table):
+def rope_table_arguments(nc, pool):
     position_int = pool.tile([P, 2], I32)
     nc.gpsimd.iota(position_int[:], pattern=[[P, 2]], base=0, channel_multiplier=1)
     position = pool.tile([P, 2], F32)
@@ -82,9 +82,7 @@ def build_rope_table(nc, pool, table):
     )
     quarter_less = pool.tile([P, width], F32)
     nc.vector.tensor_scalar_add(out=quarter_less[:], in0=minus_abs[:], scalar1=0.25)
-    nc.scalar.activation(
-        out=table[:].rearrange("p a b j e -> p (a b j e)"), in_=quarter_less[:], func=ACT.Sin, scale=TWO_PI
-    )
+    return quarter_less
 
 
 def tile_multilatentattention_pa_kernel(tc, x, Wqa_words, Wqa_scales, Wqb_words, Wqb_scales, out):
@@ -95,13 +93,14 @@ def tile_multilatentattention_pa_kernel(tc, x, Wqa_words, Wqa_scales, Wqb_words,
     with ExitStack() as ctx:
         consts = ctx.enter_context(tc.tile_pool(name="consts", bufs=1))
         grouped_pool = ctx.enter_context(tc.tile_pool(name="grouped", bufs=2))
-        codes_pool = ctx.enter_context(tc.tile_pool(name="codes", bufs=LOOKAHEAD + 1))
+        codes_pool = ctx.enter_context(tc.tile_pool(name="codes", bufs=3))
         rotate_pool = ctx.enter_context(tc.tile_pool(name="rotate", bufs=3))
         stage_pool = ctx.enter_context(tc.tile_pool(name="stage", bufs=6))
         psum_x = ctx.enter_context(tc.psum_pool(name="psum_x", bufs=2))
         psum_cq = ctx.enter_context(tc.psum_pool(name="psum_cq", bufs=1))
         psum_nope = ctx.enter_context(tc.psum_pool(name="psum_nope", bufs=2))
         psum_rope = ctx.enter_context(tc.psum_pool(name="psum_rope", bufs=3))
+        ctx.enter_context(tc.manual_schedule())
 
         wqa_planes = consts.tile([P, QL], U8, align_bytes=64)
         wqb_planes = consts.tile([P, GROUP_COLS], U8, align_bytes=64)
@@ -125,6 +124,7 @@ def tile_multilatentattention_pa_kernel(tc, x, Wqa_words, Wqa_scales, Wqb_words,
             )
 
         load_x(0)
+        load_x(1)
         for quadrant in range(4):
             rows = slice(4 * quadrant, 4 * quadrant + 4)
             live = slice(32 * quadrant, 32 * quadrant + 16)
@@ -139,7 +139,6 @@ def tile_multilatentattention_pa_kernel(tc, x, Wqa_words, Wqa_scales, Wqb_words,
         nc.sync.dma_start(
             out=wqa_words[:].bitcast(I32), in_=Wqa_words.rearrange("g p n t -> p g (n t)").bitcast(I32)
         )
-        load_x(1)
         load_wqb(0)
         load_x(2)
         for hg in range(1, HEAD_GROUPS):
@@ -147,22 +146,25 @@ def tile_multilatentattention_pa_kernel(tc, x, Wqa_words, Wqa_scales, Wqb_words,
         for i in range(3, TOKEN_TILES):
             load_x(i)
 
+        warm = consts.tile([P, 2], F32)
+        nc.vector.memset(warm[:], 0.0)
+        nc.scalar.activation(out=warm[:, 1:2], in_=warm[:, 0:1], func=ACT.Sin)
+        table_arguments = rope_table_arguments(nc, consts)
         ident_f32 = consts.tile([P, P], F32)
         make_identity(nc, ident_f32[:])
         ident_bf16 = consts.tile([P, P], BF16)
         make_identity(nc, ident_bf16[:])
         table = consts.tile([P, 2, 2, PAIRS, 2], F32)
-        build_rope_table(nc, consts, table)
 
-        def front(i):
+        live_tiles = {}
+
+        def is_tile(i):
+            return 0 <= i < TOKEN_TILES
+
+        def transpose_x(i):
+            if not is_tile(i):
+                return
             x_words = x_sb[i][:].bitcast(F32)
-            x_grouped = grouped_pool.tile([P, PASSES_A, P, PACK], BF16, align_bytes=64)
-            x_grouped_words = (
-                x_grouped[:]
-                .rearrange("p g r t -> p (g r t)")
-                .bitcast(F32)
-                .rearrange("p (g r u) -> p g r u", g=PASSES_A, u=2)
-            )
             for first in range(0, PASSES_A, 2):
                 xt = psum_x.tile([P, 2, 2, P], F32)
                 for gg in range(2):
@@ -173,17 +175,41 @@ def tile_multilatentattention_pa_kernel(tc, x, Wqa_words, Wqa_scales, Wqb_words,
                             x_words[:, start_word + u : start_word + K_PASS // 2 : 2],
                             ident_f32[:],
                         )
+                live_tiles[("xt", i, first)] = xt
+
+        def copy_x(i):
+            if not is_tile(i):
+                return
+            x_grouped = grouped_pool.tile([P, PASSES_A, P, PACK], BF16, align_bytes=64)
+            x_grouped_words = (
+                x_grouped[:]
+                .rearrange("p g r t -> p (g r t)")
+                .bitcast(F32)
+                .rearrange("p (g r u) -> p g r u", g=PASSES_A, u=2)
+            )
+            for first in range(0, PASSES_A, 2):
+                xt = live_tiles[("xt", i, first)]
                 nc.scalar.copy(
                     out=x_grouped_words[:, first : first + 2, :, :], in_=xt[:].rearrange("p g u r -> p g r u")
                 )
+            live_tiles[("x_grouped", i)] = x_grouped
+
+        def quantise_x(i):
+            if not is_tile(i):
+                return
             x_codes = codes_pool.tile([P, PASSES_A * P], U32, align_bytes=64)
             x_scales = codes_pool.tile([P, PASSES_A * P], U8, align_bytes=64)
             nc.vector.quantize_mx(
                 out=x_codes[:].bitcast(FP8X4),
                 scales=x_scales[:],
-                in_=x_grouped[:].rearrange("p g r t -> p (g r t)"),
+                in_=live_tiles[("x_grouped", i)][:].rearrange("p g r t -> p (g r t)"),
             )
+            live_tiles[("x_mx", i)] = (x_codes, x_scales)
 
+        def first_product(i):
+            if not is_tile(i):
+                return
+            x_codes, x_scales = live_tiles[("x_mx", i)]
             cq_ps = psum_cq.tile([P, QL], F32, tag="cq")
             for g in range(PASSES_A):
                 tokens = slice(g * P, (g + 1) * P)
@@ -198,11 +224,22 @@ def tile_multilatentattention_pa_kernel(tc, x, Wqa_words, Wqa_scales, Wqb_words,
                 )
             cq_bf16 = grouped_pool.tile([P, PACK, P], BF16)
             nc.scalar.copy(out=cq_bf16[:], in_=cq_ps[:].rearrange("p (c t) -> p t c", t=PACK))
+            live_tiles[("cq_bf16", i)] = cq_bf16
+
+        def transpose_cq(i):
+            if not is_tile(i):
+                return
+            cq_bf16 = live_tiles[("cq_bf16", i)]
             cqT_ps = psum_cq.tile([P, PACK, P], BF16, tag="cq")
             for t in range(PACK):
                 nc.tensor.transpose(cqT_ps[:, t, :], cq_bf16[:, t, :], ident_bf16[:])
+            live_tiles[("cqT_ps", i)] = cqT_ps
+
+        def quantise_cq(i):
+            if not is_tile(i):
+                return
             cq_grouped = grouped_pool.tile([P, P, PACK], BF16, align_bytes=64)
-            nc.scalar.copy(out=cq_grouped[:], in_=cqT_ps[:].rearrange("p t r -> p r t"))
+            nc.scalar.copy(out=cq_grouped[:], in_=live_tiles[("cqT_ps", i)][:].rearrange("p t r -> p r t"))
             cq_codes = codes_pool.tile([P, P], U32, align_bytes=64)
             cq_scales = codes_pool.tile([P, P], U8, align_bytes=64)
             nc.vector.quantize_mx(
@@ -210,9 +247,10 @@ def tile_multilatentattention_pa_kernel(tc, x, Wqa_words, Wqa_scales, Wqb_words,
                 scales=cq_scales[:],
                 in_=cq_grouped[:].rearrange("p r t -> p (r t)"),
             )
-            return cq_codes, cq_scales
+            live_tiles[("cq_mx", i)] = (cq_codes, cq_scales)
 
-        def back(i, hg, cq_codes, cq_scales):
+        def second_product_and_rope(i, hg):
+            cq_codes, cq_scales = live_tiles[("cq_mx", i)]
             half = i % (SEQ // P)
             rope_ps = psum_rope.tile([P, GROUP_HEADS, RD], F32)
             nope_ps = psum_nope.tile([P, GROUP_HEADS, ND], F32)
@@ -258,12 +296,23 @@ def tile_multilatentattention_pa_kernel(tc, x, Wqa_words, Wqa_scales, Wqb_words,
                 in_=stage[:].rearrange("p h f -> p (h f)"),
             )
 
-        ready = []
-        for i in range(LOOKAHEAD):
-            ready.append(front(i))
-        for i in range(TOKEN_TILES):
-            if i + LOOKAHEAD < TOKEN_TILES:
-                ready.append(front(i + LOOKAHEAD))
-            cq_codes, cq_scales = ready[i]
+        for i in range(-LEAD, TOKEN_TILES):
             for hg in range(HEAD_GROUPS):
-                back(i, hg, cq_codes, cq_scales)
+                if i >= 0:
+                    second_product_and_rope(i, hg)
+                if hg == 0:
+                    quantise_x(i + 2)
+                    first_product(i + 1)
+                elif hg == 2:
+                    transpose_cq(i + 1)
+                    transpose_x(i + 3)
+                    quantise_cq(i + 1)
+                elif hg == 3:
+                    copy_x(i + 3)
+            if i == -LEAD:
+                nc.scalar.activation(
+                    out=table[:].rearrange("p a b j e -> p (a b j e)"),
+                    in_=table_arguments[:],
+                    func=ACT.Sin,
+                    scale=TWO_PI,
+                )

@@ -29,6 +29,7 @@ GROUP_HEADS = 4
 HEAD_GROUPS = HEADS // GROUP_HEADS
 GROUP_COLS = GROUP_HEADS * QH
 PAIRS = RD // 2
+VECTOR_ADDS_GROUP = 0
 LEAD = 3
 
 TWO_PI = 2.0 * math.pi
@@ -285,7 +286,12 @@ def tile_multilatentattention_pa_kernel(tc, x, Wqa_words, Wqa_scales, Wqb_words,
                 in1=table[:, half, 1, :, :].unsqueeze(1).to_broadcast(shape),
                 op=ALU.mult,
             )
-            nc.gpsimd.tensor_tensor(
+            live_tiles[("rotation", i, hg)] = (stage, from_u, from_w)
+
+        def add_and_store(i, hg):
+            stage, from_u, from_w = live_tiles[("rotation", i, hg)]
+            adder = nc.vector if hg == VECTOR_ADDS_GROUP else nc.gpsimd
+            adder.tensor_tensor(
                 out=stage[:, :, ND:QH].rearrange("p h (j e) -> p h j e", e=2),
                 in0=from_u[:],
                 in1=from_w[:],
@@ -309,6 +315,8 @@ def tile_multilatentattention_pa_kernel(tc, x, Wqa_words, Wqa_scales, Wqb_words,
                     quantise_cq(i + 1)
                 elif hg == 3:
                     copy_x(i + 3)
+                if i >= 0:
+                    add_and_store(i, hg)
             if i == -LEAD:
                 nc.scalar.activation(
                     out=table[:].rearrange("p a b j e -> p (a b j e)"),

@@ -29,7 +29,6 @@ GROUP_HEADS = 4
 HEAD_GROUPS = HEADS // GROUP_HEADS
 GROUP_COLS = GROUP_HEADS * QH
 PAIRS = RD // 2
-VECTOR_ADDS_GROUP = 0
 LEAD = 3
 
 TWO_PI = 2.0 * math.pi
@@ -95,8 +94,8 @@ def tile_multilatentattention_pa_kernel(tc, x, Wqa_words, Wqa_scales, Wqb_words,
         consts = ctx.enter_context(tc.tile_pool(name="consts", bufs=1))
         grouped_pool = ctx.enter_context(tc.tile_pool(name="grouped", bufs=2))
         codes_pool = ctx.enter_context(tc.tile_pool(name="codes", bufs=3))
-        rotate_pool = ctx.enter_context(tc.tile_pool(name="rotate", bufs=3))
-        stage_pool = ctx.enter_context(tc.tile_pool(name="stage", bufs=6))
+        rotate_pool = ctx.enter_context(tc.tile_pool(name="rotate", bufs=4))
+        stage_pool = ctx.enter_context(tc.tile_pool(name="stage", bufs=8))
         psum_x = ctx.enter_context(tc.psum_pool(name="psum_x", bufs=2))
         psum_cq = ctx.enter_context(tc.psum_pool(name="psum_cq", bufs=1))
         psum_nope = ctx.enter_context(tc.psum_pool(name="psum_nope", bufs=2))
@@ -114,8 +113,11 @@ def tile_multilatentattention_pa_kernel(tc, x, Wqa_words, Wqa_scales, Wqb_words,
             x_tile = consts.tile([P, D], BF16, name="x_sb%d" % i)
             x_sb.append(x_tile)
 
-        def load_x(i):
-            nc.sync.dma_start(out=x_sb[i][:], in_=x_rows[i * P : (i + 1) * P, :])
+        def load_x(i, pieces):
+            width = D // pieces
+            for piece in range(pieces):
+                cols = slice(piece * width, (piece + 1) * width)
+                nc.sync.dma_start(out=x_sb[i][:, cols], in_=x_rows[i * P : (i + 1) * P, cols])
 
         def load_wqb(hg):
             cols = slice(hg * GROUP_COLS, (hg + 1) * GROUP_COLS)
@@ -124,8 +126,11 @@ def tile_multilatentattention_pa_kernel(tc, x, Wqa_words, Wqa_scales, Wqb_words,
                 in_=Wqb_words[0].rearrange("p n t -> p (n t)").bitcast(I32)[:, cols],
             )
 
-        load_x(0)
-        load_x(1)
+        load_x(0, 2)
+        load_x(1, 1)
+        nc.sync.dma_start(
+            out=wqa_words[:].bitcast(I32), in_=Wqa_words.rearrange("g p n t -> p g (n t)").bitcast(I32)
+        )
         for quadrant in range(4):
             rows = slice(4 * quadrant, 4 * quadrant + 4)
             live = slice(32 * quadrant, 32 * quadrant + 16)
@@ -137,15 +142,12 @@ def tile_multilatentattention_pa_kernel(tc, x, Wqa_words, Wqa_scales, Wqb_words,
                 out=wqb_planes[live, :].bitcast(I32),
                 in_=Wqb_scales[0, rows, :].rearrange("r (c n) -> c r n", c=HEAD_GROUPS).bitcast(I32),
             )
-        nc.sync.dma_start(
-            out=wqa_words[:].bitcast(I32), in_=Wqa_words.rearrange("g p n t -> p g (n t)").bitcast(I32)
-        )
         load_wqb(0)
-        load_x(2)
+        load_x(2, 1)
         for hg in range(1, HEAD_GROUPS):
             load_wqb(hg)
         for i in range(3, TOKEN_TILES):
-            load_x(i)
+            load_x(i, 1)
 
         warm = consts.tile([P, 2], F32)
         nc.vector.memset(warm[:], 0.0)
@@ -270,31 +272,24 @@ def tile_multilatentattention_pa_kernel(tc, x, Wqa_words, Wqa_scales, Wqb_words,
             stage = stage_pool.tile([P, GROUP_HEADS, QH], F32)
             nc.scalar.copy(out=stage[:, :, 0:ND], in_=nope_ps[:])
 
-            shape = [P, GROUP_HEADS, PAIRS, 2]
-            pairs = rope_ps[:].rearrange("p h (j e) -> p h j e", e=2)
-            from_u = rotate_pool.tile(shape, F32)
-            from_w = rotate_pool.tile(shape, F32)
+            shape = [P, 2, GROUP_HEADS, PAIRS, 2]
+            products = rotate_pool.tile(shape, F32)
             nc.vector.tensor_tensor(
-                out=from_u[:],
-                in0=pairs[:, :, :, 0:1].to_broadcast(shape),
-                in1=table[:, half, 0, :, :].unsqueeze(1).to_broadcast(shape),
+                out=products[:],
+                in0=rope_ps[:].rearrange("p h (j w) -> p w h j", w=2).unsqueeze(4).to_broadcast(shape),
+                in1=table[:, half].unsqueeze(2).to_broadcast(shape),
                 op=ALU.mult,
             )
-            nc.vector.tensor_tensor(
-                out=from_w[:],
-                in0=pairs[:, :, :, 1:2].to_broadcast(shape),
-                in1=table[:, half, 1, :, :].unsqueeze(1).to_broadcast(shape),
-                op=ALU.mult,
-            )
-            live_tiles[("rotation", i, hg)] = (stage, from_u, from_w)
+            live_tiles[("rotation", i, hg)] = (stage, products)
 
         def add_and_store(i, hg):
-            stage, from_u, from_w = live_tiles[("rotation", i, hg)]
-            adder = nc.vector if hg == VECTOR_ADDS_GROUP else nc.gpsimd
+            stage, products = live_tiles[("rotation", i, hg)]
+            is_last = i == TOKEN_TILES - 1 and hg == HEAD_GROUPS - 1
+            adder = nc.vector if is_last else nc.gpsimd
             adder.tensor_tensor(
                 out=stage[:, :, ND:QH].rearrange("p h (j e) -> p h j e", e=2),
-                in0=from_u[:],
-                in1=from_w[:],
+                in0=products[:, 0],
+                in1=products[:, 1],
                 op=ALU.add,
             )
             nc.sync.dma_start(

@@ -30,6 +30,7 @@ HEAD_GROUPS = HEADS // GROUP_HEADS
 GROUP_COLS = GROUP_HEADS * QH
 PAIRS = RD // 2
 LEAD = 3
+ADD_GROUPS = 2
 
 TWO_PI = 2.0 * math.pi
 ROUND_MAGIC = 1.5 * 2.0**23
@@ -95,7 +96,7 @@ def tile_multilatentattention_pa_kernel(tc, x, Wqa_words, Wqa_scales, Wqb_words,
         grouped_pool = ctx.enter_context(tc.tile_pool(name="grouped", bufs=2))
         codes_pool = ctx.enter_context(tc.tile_pool(name="codes", bufs=3))
         rotate_pool = ctx.enter_context(tc.tile_pool(name="rotate", bufs=4))
-        stage_pool = ctx.enter_context(tc.tile_pool(name="stage", bufs=8))
+        stage_pool = ctx.enter_context(tc.tile_pool(name="stage", bufs=5))
         psum_x = ctx.enter_context(tc.psum_pool(name="psum_x", bufs=2))
         psum_cq = ctx.enter_context(tc.psum_pool(name="psum_cq", bufs=1))
         psum_nope = ctx.enter_context(tc.psum_pool(name="psum_nope", bufs=2))
@@ -269,33 +270,47 @@ def tile_multilatentattention_pa_kernel(tc, x, Wqa_words, Wqa_scales, Wqb_words,
                         start=True,
                         stop=True,
                     )
-            stage = stage_pool.tile([P, GROUP_HEADS, QH], F32)
-            nc.scalar.copy(out=stage[:, :, 0:ND], in_=nope_ps[:])
+            first_group = hg - hg % ADD_GROUPS
+            if hg == first_group:
+                stage = stage_pool.tile([P, ADD_GROUPS * GROUP_HEADS, QH], F32)
+                products = rotate_pool.tile([P, 2, ADD_GROUPS * GROUP_HEADS, PAIRS, 2], F32)
+                live_tiles[("rotation", i, first_group)] = (stage, products)
+            stage, products = live_tiles[("rotation", i, first_group)]
+            heads_here = slice((hg - first_group) * GROUP_HEADS, (hg - first_group + 1) * GROUP_HEADS)
+            nc.scalar.copy(out=stage[:, heads_here, 0:ND], in_=nope_ps[:])
 
             shape = [P, 2, GROUP_HEADS, PAIRS, 2]
-            products = rotate_pool.tile(shape, F32)
             nc.vector.tensor_tensor(
-                out=products[:],
+                out=products[:, :, heads_here],
                 in0=rope_ps[:].rearrange("p h (j w) -> p w h j", w=2).unsqueeze(4).to_broadcast(shape),
                 in1=table[:, half].unsqueeze(2).to_broadcast(shape),
                 op=ALU.mult,
             )
-            live_tiles[("rotation", i, hg)] = (stage, products)
 
         def add_and_store(i, hg):
-            stage, products = live_tiles[("rotation", i, hg)]
-            is_last = i == TOKEN_TILES - 1 and hg == HEAD_GROUPS - 1
-            adder = nc.vector if is_last else nc.gpsimd
+            first_group = hg - hg % ADD_GROUPS
+            stage, products = live_tiles[("rotation", i, first_group)]
+            at_end = i == TOKEN_TILES - 1 and first_group == HEAD_GROUPS - ADD_GROUPS
+            if at_end:
+                groups = [hg]
+            elif hg == first_group + ADD_GROUPS - 1:
+                groups = list(range(first_group, hg + 1))
+            else:
+                return
+            adder = nc.vector if at_end and hg == HEAD_GROUPS - 1 else nc.gpsimd
+            heads = slice((groups[0] - first_group) * GROUP_HEADS, (groups[-1] - first_group + 1) * GROUP_HEADS)
             adder.tensor_tensor(
-                out=stage[:, :, ND:QH].rearrange("p h (j e) -> p h j e", e=2),
-                in0=products[:, 0],
-                in1=products[:, 1],
+                out=stage[:, heads, ND:QH].rearrange("p h (j e) -> p h j e", e=2),
+                in0=products[:, 0, heads],
+                in1=products[:, 1, heads],
                 op=ALU.add,
             )
-            nc.sync.dma_start(
-                out=out_rows[i * P : (i + 1) * P, hg * GROUP_COLS : (hg + 1) * GROUP_COLS],
-                in_=stage[:].rearrange("p h f -> p (h f)"),
-            )
+            for group in groups:
+                heads = slice((group - first_group) * GROUP_HEADS, (group - first_group + 1) * GROUP_HEADS)
+                nc.sync.dma_start(
+                    out=out_rows[i * P : (i + 1) * P, group * GROUP_COLS : (group + 1) * GROUP_COLS],
+                    in_=stage[:, heads, :].rearrange("p h f -> p (h f)"),
+                )
 
         for i in range(-LEAD, TOKEN_TILES):
             for hg in range(HEAD_GROUPS):

@@ -29,8 +29,10 @@ GROUP_HEADS = 4
 HEAD_GROUPS = HEADS // GROUP_HEADS
 GROUP_COLS = GROUP_HEADS * QH
 PAIRS = RD // 2
+STEPS = TOKEN_TILES * HEAD_GROUPS
 LEAD = 3
 ADD_GROUPS = 2
+SINGLE_AT_END = 3
 
 TWO_PI = 2.0 * math.pi
 ROUND_MAGIC = 1.5 * 2.0**23
@@ -253,6 +255,12 @@ def tile_multilatentattention_pa_kernel(tc, x, Wqa_words, Wqa_scales, Wqb_words,
             )
             live_tiles[("cq_mx", i)] = (cq_codes, cq_scales)
 
+        def add_unit(step):
+            if step == 0 or step >= STEPS - SINGLE_AT_END:
+                return [step]
+            first = step - (step + 1) % ADD_GROUPS
+            return [first, first + 1]
+
         def second_product_and_rope(i, hg):
             cq_codes, cq_scales = live_tiles[("cq_mx", i)]
             half = i % (SEQ // P)
@@ -270,13 +278,14 @@ def tile_multilatentattention_pa_kernel(tc, x, Wqa_words, Wqa_scales, Wqb_words,
                         start=True,
                         stop=True,
                     )
-            first_group = hg - hg % ADD_GROUPS
-            if hg == first_group:
+            step = i * HEAD_GROUPS + hg
+            unit = add_unit(step)
+            if step == unit[0]:
                 stage = stage_pool.tile([P, ADD_GROUPS * GROUP_HEADS, QH], F32)
                 products = rotate_pool.tile([P, 2, ADD_GROUPS * GROUP_HEADS, PAIRS, 2], F32)
-                live_tiles[("rotation", i, first_group)] = (stage, products)
-            stage, products = live_tiles[("rotation", i, first_group)]
-            heads_here = slice((hg - first_group) * GROUP_HEADS, (hg - first_group + 1) * GROUP_HEADS)
+                live_tiles[("rotation", unit[0])] = (stage, products)
+            stage, products = live_tiles[("rotation", unit[0])]
+            heads_here = slice((step - unit[0]) * GROUP_HEADS, (step - unit[0] + 1) * GROUP_HEADS)
             nc.scalar.copy(out=stage[:, heads_here, 0:ND], in_=nope_ps[:])
 
             shape = [P, 2, GROUP_HEADS, PAIRS, 2]
@@ -288,28 +297,24 @@ def tile_multilatentattention_pa_kernel(tc, x, Wqa_words, Wqa_scales, Wqb_words,
             )
 
         def add_and_store(i, hg):
-            first_group = hg - hg % ADD_GROUPS
-            stage, products = live_tiles[("rotation", i, first_group)]
-            at_end = i == TOKEN_TILES - 1 and first_group == HEAD_GROUPS - ADD_GROUPS
-            if at_end:
-                groups = [hg]
-            elif hg == first_group + ADD_GROUPS - 1:
-                groups = list(range(first_group, hg + 1))
-            else:
+            step = i * HEAD_GROUPS + hg
+            unit = add_unit(step)
+            if step != unit[-1]:
                 return
-            adder = nc.vector if at_end and hg == HEAD_GROUPS - 1 else nc.gpsimd
-            heads = slice((groups[0] - first_group) * GROUP_HEADS, (groups[-1] - first_group + 1) * GROUP_HEADS)
+            stage, products = live_tiles[("rotation", unit[0])]
+            adder = nc.vector if step == STEPS - 1 else nc.gpsimd
+            heads = slice(0, len(unit) * GROUP_HEADS)
             adder.tensor_tensor(
                 out=stage[:, heads, ND:QH].rearrange("p h (j e) -> p h j e", e=2),
                 in0=products[:, 0, heads],
                 in1=products[:, 1, heads],
                 op=ALU.add,
             )
-            for group in groups:
-                heads = slice((group - first_group) * GROUP_HEADS, (group - first_group + 1) * GROUP_HEADS)
+            for place, member in enumerate(unit):
+                tile_of, group = divmod(member, HEAD_GROUPS)
                 nc.sync.dma_start(
-                    out=out_rows[i * P : (i + 1) * P, group * GROUP_COLS : (group + 1) * GROUP_COLS],
-                    in_=stage[:, heads, :].rearrange("p h f -> p (h f)"),
+                    out=out_rows[tile_of * P : (tile_of + 1) * P, group * GROUP_COLS : (group + 1) * GROUP_COLS],
+                    in_=stage[:, place * GROUP_HEADS : (place + 1) * GROUP_HEADS, :].rearrange("p h f -> p (h f)"),
                 )
 
         for i in range(-LEAD, TOKEN_TILES):

@@ -138,6 +138,7 @@ def tile_multilatentattention_pa_kernel(tc, x, Wqa_words, Wqa_scales, Wqb_words,
             rows = slice(4 * quadrant, 4 * quadrant + 4)
             live = slice(32 * quadrant, 32 * quadrant + 16)
             nc.sync.dma_start(out=wqa_planes[live, :].bitcast(I32), in_=Wqa_scales[:, rows, :].bitcast(I32))
+        load_x(2, 1)
         for quadrant in range(4):
             rows = slice(4 * quadrant, 4 * quadrant + 4)
             live = slice(32 * quadrant, 32 * quadrant + 16)
@@ -146,7 +147,6 @@ def tile_multilatentattention_pa_kernel(tc, x, Wqa_words, Wqa_scales, Wqb_words,
                 in_=Wqb_scales[0, rows, :].rearrange("r (c n) -> c r n", c=HEAD_GROUPS).bitcast(I32),
             )
         load_wqb(0)
-        load_x(2, 1)
         for hg in range(1, HEAD_GROUPS):
             load_wqb(hg)
         for i in range(3, TOKEN_TILES):
@@ -326,9 +326,9 @@ def tile_multilatentattention_pa_kernel(tc, x, Wqa_words, Wqa_scales, Wqb_words,
                     first_product(i + 1)
                 elif hg == 2:
                     transpose_cq(i + 1)
-                    transpose_x(i + 3)
                     quantise_cq(i + 1)
                 elif hg == 3:
+                    transpose_x(i + 3)
                     copy_x(i + 3)
                 if i >= 0:
                     add_and_store(i, hg)

@@ -130,14 +130,14 @@ def tile_multilatentattention_pa_kernel(tc, x, Wqa_words, Wqa_scales, Wqb_words,
             )
 
         load_x(0, 2)
-        load_x(1, 1)
-        nc.sync.dma_start(
-            out=wqa_words[:].bitcast(I32), in_=Wqa_words.rearrange("g p n t -> p g (n t)").bitcast(I32)
-        )
         for quadrant in range(4):
             rows = slice(4 * quadrant, 4 * quadrant + 4)
             live = slice(32 * quadrant, 32 * quadrant + 16)
             nc.sync.dma_start(out=wqa_planes[live, :].bitcast(I32), in_=Wqa_scales[:, rows, :].bitcast(I32))
+        load_x(1, 1)
+        nc.sync.dma_start(
+            out=wqa_words[:].bitcast(I32), in_=Wqa_words.rearrange("g p n t -> p g (n t)").bitcast(I32)
+        )
         load_x(2, 1)
         for quadrant in range(4):
             rows = slice(4 * quadrant, 4 * quadrant + 4)

@@ -32,7 +32,8 @@ PAIRS = RD // 2
 STEPS = TOKEN_TILES * HEAD_GROUPS
 LEAD = 3
 ADD_GROUPS = 2
-SINGLE_AT_END = 3
+LAST_QUANTISE_STEP = STEPS - HEAD_GROUPS - 2
+SINGLE_AT_END = STEPS - 1 - LAST_QUANTISE_STEP
 
 TWO_PI = 2.0 * math.pi
 ROUND_MAGIC = 1.5 * 2.0**23
@@ -302,7 +303,7 @@ def tile_multilatentattention_pa_kernel(tc, x, Wqa_words, Wqa_scales, Wqb_words,
             if step != unit[-1]:
                 return
             stage, products = live_tiles[("rotation", unit[0])]
-            adder = nc.vector if step == STEPS - 1 else nc.gpsimd
+            adder = nc.vector if step in (LAST_QUANTISE_STEP, STEPS - 1) else nc.gpsimd
             heads = slice(0, len(unit) * GROUP_HEADS)
             adder.tensor_tensor(
                 out=stage[:, heads, ND:QH].rearrange("p h (j e) -> p h j e", e=2),

@@ -31,6 +31,8 @@ GROUP_COLS = GROUP_HEADS * QH
 PAIRS = RD // 2
 STEPS = TOKEN_TILES * HEAD_GROUPS
 LEAD = 3
+WARM_FIRST = 4
+WARM_BEHIND_X = (2, 4)
 ADD_GROUPS = 2
 LAST_QUANTISE_STEP = STEPS - HEAD_GROUPS - 2
 SINGLE_AT_END = STEPS - 1 - LAST_QUANTISE_STEP
@@ -106,6 +108,9 @@ def tile_multilatentattention_pa_kernel(tc, x, Wqa_words, Wqa_scales, Wqb_words,
         psum_rope = ctx.enter_context(tc.psum_pool(name="psum_rope", bufs=3))
         ctx.enter_context(tc.manual_schedule())
 
+        zeros = consts.tile([P, QL], BF16)
+        nc.vector.memset(zeros[:], 0.0)
+
         wqa_planes = consts.tile([P, QL], U8, align_bytes=64)
         wqb_planes = consts.tile([P, GROUP_COLS], U8, align_bytes=64)
         nc.vector.memset(wqa_planes[:].bitcast(I32), 0)
@@ -164,6 +169,13 @@ def tile_multilatentattention_pa_kernel(tc, x, Wqa_words, Wqa_scales, Wqb_words,
         table = consts.tile([P, 2, 2, PAIRS, 2], F32)
 
         live_tiles = {}
+
+        def keep_tensor_engine_busy(passes):
+            idle_ps = psum_nope.tile([P, GROUP_HEADS, ND], F32, tag="nope_ps")
+            for unused in range(passes):
+                nc.tensor.matmul(
+                    out=idle_ps[:].rearrange("p h f -> p (h f)"), lhsT=zeros[:, 0:P], rhs=zeros[:], start=True, stop=True
+                )
 
         def is_tile(i):
             return 0 <= i < TOKEN_TILES
@@ -318,6 +330,7 @@ def tile_multilatentattention_pa_kernel(tc, x, Wqa_words, Wqa_scales, Wqb_words,
                     in_=stage[:, place * GROUP_HEADS : (place + 1) * GROUP_HEADS, :].rearrange("p h f -> p (h f)"),
                 )
 
+        keep_tensor_engine_busy(WARM_FIRST)
         for i in range(-LEAD, TOKEN_TILES):
             for hg in range(HEAD_GROUPS):
                 if i >= 0:
@@ -331,6 +344,8 @@ def tile_multilatentattention_pa_kernel(tc, x, Wqa_words, Wqa_scales, Wqb_words,
                 elif hg == 3:
                     transpose_x(i + 3)
                     copy_x(i + 3)
+                    if i + 3 < len(WARM_BEHIND_X):
+                        keep_tensor_engine_busy(WARM_BEHIND_X[i + 3])
                 if i >= 0:
                     add_and_store(i, hg)
             if i == -LEAD:

@@ -31,7 +31,8 @@ GROUP_COLS = GROUP_HEADS * QH
 PAIRS = RD // 2
 STEPS = TOKEN_TILES * HEAD_GROUPS
 LEAD = 3
-WARM_FIRST = 4
+WARM_FIRST = 6
+WARM_BEHIND_FIRST_PRODUCT = 3
 WARM_BEHIND_X = (2, 4)
 ADD_GROUPS = 2
 LAST_QUANTISE_STEP = STEPS - HEAD_GROUPS - 2
@@ -338,6 +339,8 @@ def tile_multilatentattention_pa_kernel(tc, x, Wqa_words, Wqa_scales, Wqb_words,
                 if hg == 0:
                     quantise_x(i + 2)
                     first_product(i + 1)
+                    if i + 1 == 0:
+                        keep_tensor_engine_busy(WARM_BEHIND_FIRST_PRODUCT)
                 elif hg == 2:
                     transpose_cq(i + 1)
                     quantise_cq(i + 1)

import math
from contextlib import ExitStack

import concourse.mybir as mybir
from concourse.masks import make_identity

F32 = mybir.dt.float32
BF16 = mybir.dt.bfloat16
I32 = mybir.dt.int32
U32 = mybir.dt.uint32
U8 = mybir.dt.uint8
FP8X4 = mybir.dt.float8_e4m3fn_x4
ALU = mybir.AluOpType
ACT = mybir.ActivationFunctionType

P = 128
PACK = 4
K_PASS = P * PACK

TOKENS, D, QL = 1024, 2048, 512
HEADS, ND, RD = 16, 128, 128
QH = ND + RD
SEQ = 256
BASE = 10000.0

TOKEN_TILES = TOKENS // P
PASSES_A = D // K_PASS
GROUP_HEADS = 4
HEAD_GROUPS = HEADS // GROUP_HEADS
GROUP_COLS = GROUP_HEADS * QH
PAIRS = RD // 2
STEPS = TOKEN_TILES * HEAD_GROUPS
LEAD = 3
WARM_FIRST = 6
WARM_BEHIND_FIRST_PRODUCT = 3
WARM_BEHIND_X = (2, 4)
ADD_GROUPS = 2
LAST_QUANTISE_STEP = STEPS - HEAD_GROUPS - 2
SINGLE_AT_END = STEPS - 1 - LAST_QUANTISE_STEP

TWO_PI = 2.0 * math.pi
ROUND_MAGIC = 1.5 * 2.0**23

FLOPS = 2 * TOKENS * D * QL + 2 * TOKENS * QL * HEADS * QH


def rope_table_arguments(nc, pool):
    position_int = pool.tile([P, 2], I32)
    nc.gpsimd.iota(position_int[:], pattern=[[P, 2]], base=0, channel_multiplier=1)
    position = pool.tile([P, 2], F32)
    nc.vector.tensor_copy(out=position[:], in_=position_int[:])

    freq = pool.tile([P, PAIRS], F32)
    nc.vector.memset(freq[:], 1.0)
    step = 1
    while step < PAIRS:
        bit_set = freq[:].rearrange("p (a two c) -> p a two c", two=2, c=step)[:, :, 1, :]
        nc.vector.tensor_scalar_mul(out=bit_set, in0=bit_set, scalar1=BASE ** (-2.0 * step / RD))
        step *= 2

    turns = pool.tile([P, 2, PAIRS], F32)
    for half in range(2):
        nc.vector.tensor_scalar(
            out=turns[:, half, :],
            in0=freq[:],
            scalar1=position[:, half : half + 1],
            scalar2=1.0 / TWO_PI,
            op0=ALU.mult,
            op1=ALU.mult,
        )

    shifted = pool.tile([P, 2, 2, PAIRS, 2], F32)
    nc.vector.tensor_copy(out=shifted[:, :, 0, :, 0], in_=turns[:])
    nc.vector.tensor_scalar_add(out=shifted[:, :, 0, :, 1], in0=turns[:], scalar1=-0.25)
    nc.vector.tensor_scalar_add(out=shifted[:, :, 1, :, 0], in0=turns[:], scalar1=0.25)
    nc.vector.tensor_copy(out=shifted[:, :, 1, :, 1], in_=turns[:])
    shifted_flat = shifted[:].rearrange("p a b j e -> p (a b j e)")

    width = 2 * 2 * PAIRS * 2
    whole = pool.tile([P, width], F32)
    nc.vector.tensor_scalar(
        out=whole[:], in0=shifted_flat, scalar1=ROUND_MAGIC, scalar2=ROUND_MAGIC, op0=ALU.add, op1=ALU.subtract
    )
    part = pool.tile([P, width], F32)
    nc.vector.tensor_tensor(out=part[:], in0=shifted_flat, in1=whole[:], op=ALU.subtract)
    minus_abs = pool.tile([P, width], F32)
    nc.vector.scalar_tensor_tensor(
        out=minus_abs[:], in0=part[:], scalar=-1.0, in1=part[:], op0=ALU.mult, op1=ALU.min
    )
    quarter_less = pool.tile([P, width], F32)
    nc.vector.tensor_scalar_add(out=quarter_less[:], in0=minus_abs[:], scalar1=0.25)
    return quarter_less


def tile_multilatentattention_pa_kernel(tc, x, Wqa_words, Wqa_scales, Wqb_words, Wqb_scales, out):
    nc = tc.nc
    x_rows = x.rearrange("b s d -> (b s) d")
    out_rows = out.rearrange("b s h f -> (b s) (h f)")

    with ExitStack() as ctx:
        consts = ctx.enter_context(tc.tile_pool(name="consts", bufs=1))
        grouped_pool = ctx.enter_context(tc.tile_pool(name="grouped", bufs=2))
        codes_pool = ctx.enter_context(tc.tile_pool(name="codes", bufs=3))
        rotate_pool = ctx.enter_context(tc.tile_pool(name="rotate", bufs=4))
        stage_pool = ctx.enter_context(tc.tile_pool(name="stage", bufs=5))
        psum_x = ctx.enter_context(tc.psum_pool(name="psum_x", bufs=2))
        psum_cq = ctx.enter_context(tc.psum_pool(name="psum_cq", bufs=1))
        psum_nope = ctx.enter_context(tc.psum_pool(name="psum_nope", bufs=2))
        psum_rope = ctx.enter_context(tc.psum_pool(name="psum_rope", bufs=3))
        ctx.enter_context(tc.manual_schedule())

        zeros = consts.tile([P, QL], BF16)
        nc.vector.memset(zeros[:], 0.0)

        wqa_planes = consts.tile([P, QL], U8, align_bytes=64)
        wqb_planes = consts.tile([P, GROUP_COLS], U8, align_bytes=64)
        nc.vector.memset(wqa_planes[:].bitcast(I32), 0)
        nc.vector.memset(wqb_planes[:].bitcast(I32), 0)
        wqa_words = consts.tile([P, PASSES_A, QL], U32, align_bytes=64)
        wqb_words = consts.tile([P, HEADS * QH], U32, align_bytes=64)
        x_sb = []
        for i in range(TOKEN_TILES):
            x_tile = consts.tile([P, D], BF16, name="x_sb%d" % i)
            x_sb.append(x_tile)

        def load_x(i, pieces):
            width = D // pieces
            for piece in range(pieces):
                cols = slice(piece * width, (piece + 1) * width)
                nc.sync.dma_start(out=x_sb[i][:, cols], in_=x_rows[i * P : (i + 1) * P, cols])

        def load_wqb(hg):
            cols = slice(hg * GROUP_COLS, (hg + 1) * GROUP_COLS)
            nc.sync.dma_start(
                out=wqb_words[:, cols].bitcast(I32),
                in_=Wqb_words[0].rearrange("p n t -> p (n t)").bitcast(I32)[:, cols],
            )

        load_x(0, 2)
        for quadrant in range(4):
            rows = slice(4 * quadrant, 4 * quadrant + 4)
            live = slice(32 * quadrant, 32 * quadrant + 16)
            nc.sync.dma_start(out=wqa_planes[live, :].bitcast(I32), in_=Wqa_scales[:, rows, :].bitcast(I32))
        load_x(1, 1)
        nc.sync.dma_start(
            out=wqa_words[:].bitcast(I32), in_=Wqa_words.rearrange("g p n t -> p g (n t)").bitcast(I32)
        )
        load_x(2, 1)
        for quadrant in range(4):
            rows = slice(4 * quadrant, 4 * quadrant + 4)
            live = slice(32 * quadrant, 32 * quadrant + 16)
            nc.sync.dma_start(
                out=wqb_planes[live, :].bitcast(I32),
                in_=Wqb_scales[0, rows, :].rearrange("r (c n) -> c r n", c=HEAD_GROUPS).bitcast(I32),
            )
        load_wqb(0)
        for hg in range(1, HEAD_GROUPS):
            load_wqb(hg)
        for i in range(3, TOKEN_TILES):
            load_x(i, 1)

        warm = consts.tile([P, 2], F32)
        nc.vector.memset(warm[:], 0.0)
        nc.scalar.activation(out=warm[:, 1:2], in_=warm[:, 0:1], func=ACT.Sin)
        table_arguments = rope_table_arguments(nc, consts)
        ident_f32 = consts.tile([P, P], F32)
        make_identity(nc, ident_f32[:])
        ident_bf16 = consts.tile([P, P], BF16)
        make_identity(nc, ident_bf16[:])
        table = consts.tile([P, 2, 2, PAIRS, 2], F32)

        live_tiles = {}

        def keep_tensor_engine_busy(passes):
            idle_ps = psum_nope.tile([P, GROUP_HEADS, ND], F32, tag="nope_ps")
            for unused in range(passes):
                nc.tensor.matmul(
                    out=idle_ps[:].rearrange("p h f -> p (h f)"), lhsT=zeros[:, 0:P], rhs=zeros[:], start=True, stop=True
                )

        def is_tile(i):
            return 0 <= i < TOKEN_TILES

        def transpose_x(i):
            if not is_tile(i):
                return
            x_words = x_sb[i][:].bitcast(F32)
            for first in range(0, PASSES_A, 2):
                xt = psum_x.tile([P, 2, 2, P], F32)
                for gg in range(2):
                    start_word = (first + gg) * (K_PASS // 2)
                    for u in range(2):
                        nc.tensor.transpose(
                            xt[:, gg, u, :],
                            x_words[:, start_word + u : start_word + K_PASS // 2 : 2],
                            ident_f32[:],
                        )
                live_tiles[("xt", i, first)] = xt

        def copy_x(i):
            if not is_tile(i):
                return
            x_grouped = grouped_pool.tile([P, PASSES_A, P, PACK], BF16, align_bytes=64)
            x_grouped_words = (
                x_grouped[:]
                .rearrange("p g r t -> p (g r t)")
                .bitcast(F32)
                .rearrange("p (g r u) -> p g r u", g=PASSES_A, u=2)
            )
            for first in range(0, PASSES_A, 2):
                xt = live_tiles[("xt", i, first)]
                nc.scalar.copy(
                    out=x_grouped_words[:, first : first + 2, :, :], in_=xt[:].rearrange("p g u r -> p g r u")
                )
            live_tiles[("x_grouped", i)] = x_grouped

        def quantise_x(i):
            if not is_tile(i):
                return
            x_codes = codes_pool.tile([P, PASSES_A * P], U32, align_bytes=64)
            x_scales = codes_pool.tile([P, PASSES_A * P], U8, align_bytes=64)
            nc.vector.quantize_mx(
                out=x_codes[:].bitcast(FP8X4),
                scales=x_scales[:],
                in_=live_tiles[("x_grouped", i)][:].rearrange("p g r t -> p (g r t)"),
            )
            live_tiles[("x_mx", i)] = (x_codes, x_scales)

        def first_product(i):
            if not is_tile(i):
                return
            x_codes, x_scales = live_tiles[("x_mx", i)]
            cq_ps = psum_cq.tile([P, QL], F32, tag="cq")
            for g in range(PASSES_A):
                tokens = slice(g * P, (g + 1) * P)
                nc.tensor.matmul_mx(
                    out=cq_ps[:],
                    lhsT=x_codes[:, tokens].bitcast(FP8X4),
                    lhsT_scale=x_scales[:, tokens],
                    rhs=wqa_words[:, g, :].bitcast(FP8X4),
                    rhs_scale=wqa_planes[4 * g : P, :],
                    start=(g == 0),
                    stop=(g == PASSES_A - 1),
                )
            cq_bf16 = grouped_pool.tile([P, PACK, P], BF16)
            nc.scalar.copy(out=cq_bf16[:], in_=cq_ps[:].rearrange("p (c t) -> p t c", t=PACK))
            live_tiles[("cq_bf16", i)] = cq_bf16

        def transpose_cq(i):
            if not is_tile(i):
                return
            cq_bf16 = live_tiles[("cq_bf16", i)]
            cqT_ps = psum_cq.tile([P, PACK, P], BF16, tag="cq")
            for t in range(PACK):
                nc.tensor.transpose(cqT_ps[:, t, :], cq_bf16[:, t, :], ident_bf16[:])
            live_tiles[("cqT_ps", i)] = cqT_ps

        def quantise_cq(i):
            if not is_tile(i):
                return
            cq_grouped = grouped_pool.tile([P, P, PACK], BF16, align_bytes=64)
            nc.scalar.copy(out=cq_grouped[:], in_=live_tiles[("cqT_ps", i)][:].rearrange("p t r -> p r t"))
            cq_codes = codes_pool.tile([P, P], U32, align_bytes=64)
            cq_scales = codes_pool.tile([P, P], U8, align_bytes=64)
            nc.vector.quantize_mx(
                out=cq_codes[:].bitcast(FP8X4),
                scales=cq_scales[:],
                in_=cq_grouped[:].rearrange("p r t -> p (r t)"),
            )
            live_tiles[("cq_mx", i)] = (cq_codes, cq_scales)

        def add_unit(step):
            if step == 0 or step >= STEPS - SINGLE_AT_END:
                return [step]
            first = step - (step + 1) % ADD_GROUPS
            return [first, first + 1]

        def second_product_and_rope(i, hg):
            cq_codes, cq_scales = live_tiles[("cq_mx", i)]
            half = i % (SEQ // P)
            rope_ps = psum_rope.tile([P, GROUP_HEADS, RD], F32)
            nope_ps = psum_nope.tile([P, GROUP_HEADS, ND], F32)
            for bank, offset in ((rope_ps, ND), (nope_ps, 0)):
                for hh in range(GROUP_HEADS):
                    first = hh * QH + offset
                    nc.tensor.matmul_mx(
                        out=bank[:, hh, :],
                        lhsT=cq_codes[:].bitcast(FP8X4),
                        lhsT_scale=cq_scales[:],
                        rhs=wqb_words[:, hg * GROUP_COLS + first : hg * GROUP_COLS + first + P].bitcast(FP8X4),
                        rhs_scale=wqb_planes[4 * hg : P, first : first + P],
                        start=True,
                        stop=True,
                    )
            step = i * HEAD_GROUPS + hg
            unit = add_unit(step)
            if step == unit[0]:
                stage = stage_pool.tile([P, ADD_GROUPS * GROUP_HEADS, QH], F32)
                products = rotate_pool.tile([P, 2, ADD_GROUPS * GROUP_HEADS, PAIRS, 2], F32)
                live_tiles[("rotation", unit[0])] = (stage, products)
            stage, products = live_tiles[("rotation", unit[0])]
            heads_here = slice((step - unit[0]) * GROUP_HEADS, (step - unit[0] + 1) * GROUP_HEADS)
            nc.scalar.copy(out=stage[:, heads_here, 0:ND], in_=nope_ps[:])

            shape = [P, 2, GROUP_HEADS, PAIRS, 2]
            nc.vector.tensor_tensor(
                out=products[:, :, heads_here],
                in0=rope_ps[:].rearrange("p h (j w) -> p w h j", w=2).unsqueeze(4).to_broadcast(shape),
                in1=table[:, half].unsqueeze(2).to_broadcast(shape),
                op=ALU.mult,
            )

        def add_and_store(i, hg):
            step = i * HEAD_GROUPS + hg
            unit = add_unit(step)
            if step != unit[-1]:
                return
            stage, products = live_tiles[("rotation", unit[0])]
            adder = nc.vector if step in (LAST_QUANTISE_STEP, STEPS - 1) else nc.gpsimd
            heads = slice(0, len(unit) * GROUP_HEADS)
            adder.tensor_tensor(
                out=stage[:, heads, ND:QH].rearrange("p h (j e) -> p h j e", e=2),
                in0=products[:, 0, heads],
                in1=products[:, 1, heads],
                op=ALU.add,
            )
            for place, member in enumerate(unit):
                tile_of, group = divmod(member, HEAD_GROUPS)
                nc.sync.dma_start(
                    out=out_rows[tile_of * P : (tile_of + 1) * P, group * GROUP_COLS : (group + 1) * GROUP_COLS],
                    in_=stage[:, place * GROUP_HEADS : (place + 1) * GROUP_HEADS, :].rearrange("p h f -> p (h f)"),
                )

        keep_tensor_engine_busy(WARM_FIRST)
        for i in range(-LEAD, TOKEN_TILES):
            for hg in range(HEAD_GROUPS):
                if i >= 0:
                    second_product_and_rope(i, hg)
                if hg == 0:
                    quantise_x(i + 2)
                    first_product(i + 1)
                    if i + 1 == 0:
                        keep_tensor_engine_busy(WARM_BEHIND_FIRST_PRODUCT)
                elif hg == 2:
                    transpose_cq(i + 1)
                    quantise_cq(i + 1)
                elif hg == 3:
                    transpose_x(i + 3)
                    copy_x(i + 3)
                    if i + 3 < len(WARM_BEHIND_X):
                        keep_tensor_engine_busy(WARM_BEHIND_X[i + 3])
                if i >= 0:
                    add_and_store(i, hg)
            if i == -LEAD:
                nc.scalar.activation(
                    out=table[:].rearrange("p a b j e -> p (a b j e)"),
                    in_=table_arguments[:],
                    func=ACT.Sin,
                    scale=TWO_PI,
                )
